import numpy as np
import ml_dtypes


def mxq(x, axis, fmt="e4m3"):
    dtype, down = {"e4m3": (ml_dtypes.float8_e4m3fn, 7), "e5m2": (ml_dtypes.float8_e5m2, 14)}[fmt]
    v = np.moveaxis(np.asarray(x, np.float32).astype(ml_dtypes.bfloat16).astype(np.float64), axis, -1)
    blocks = v.reshape(v.shape[:-1] + (-1, 32))
    amax = np.abs(blocks).max(-1, keepdims=True)
    byte = np.maximum(np.where(amax > 0, np.frexp(amax)[1] - 1 + 127, 0) - down, 1)
    scale = np.exp2(byte - 127.0)
    codes = (blocks / scale).astype(np.float32).astype(dtype).astype(np.float64)
    return np.moveaxis((codes * scale).reshape(v.shape), -1, axis)


WIDE = False


def mx_kscale(k):
    if not WIDE:
        return np.ones(k)
    levels = np.array([10, -10, 5, -5, 0])
    a = np.random.permutation(np.resize(levels, k // 512 * 4)).reshape(k // 512, 4)
    idx = np.arange(k)
    return np.exp2(a[idx // 512, idx % 128 // 32])


BF16 = ml_dtypes.bfloat16


def bf(x):
    return np.asarray(x, np.float32).astype(BF16)


def f64(x):
    return np.asarray(x).astype(np.float64)


NSMP, NA, DOUT, REALNA = 512, 512, 128, 520


def setup_inputs():
    s = mx_kscale(NA)
    inp = np.random.uniform(0.0, 1.0, (NSMP, REALNA + NSMP))
    g = 0.2 + 1.8 * np.random.uniform(0.0, 1.0, NSMP)
    inp[:, REALNA - 8:REALNA + NSMP - 8] *= g
    inp[:, :NA] = np.random.standard_normal((NSMP, NA)) * s
    return {"input": bf(inp), "weight": bf(np.random.standard_normal((NA, DOUT)) * 6.0 / np.sqrt(NA) / s[:, None])}


def reference(input, weight):
    inp = f64(input)
    nSmp = NSMP
    na = NA
    X = inp[:, :na]
    realna = inp.shape[1] - nSmp
    A = inp[:, realna - 8:realna + nSmp - 8]
    A = A + np.eye(nSmp)
    d = np.sum(A, axis=0)
    d_inv_sqrt = 1.0 / np.sqrt(d)
    DAD = d_inv_sqrt[:, None] * A * d_inv_sqrt[None, :]
    support = mxq(X, 1, "e4m3") @ mxq(f64(weight), 0, "e4m3")
    output = mxq(DAD, 1, "e4m3") @ mxq(support, 0, "e4m3")
    return np.concatenate((output, A), axis=1)

@@ -1,0 +1,169 @@
+from contextlib import ExitStack
+
+import concourse.mybir as mybir
+from concourse.masks import make_identity
+
+F32 = mybir.dt.float32
+BF16 = mybir.dt.bfloat16
+U32 = mybir.dt.uint32
+U8 = mybir.dt.uint8
+FP8X4 = mybir.dt.float8_e4m3fn_x4
+ALU = mybir.AluOpType
+ACT = mybir.ActivationFunctionType
+
+P = 128
+PACK = 4
+NODES = 512
+FEATS = 512
+DOUT = 128
+CHUNKS = NODES // P
+
+FLOPS = 2 * NODES * FEATS * DOUT + 2 * NODES * NODES * DOUT
+
+
+def tile_crossviewgcn_layer1_s_kernel(tc, inp, weight, out):
+    nc = tc.nc
+    with ExitStack() as ctx:
+        keep = ctx.enter_context(tc.tile_pool(name="keep", bufs=1))
+        psum = ctx.enter_context(tc.psum_pool(name="psum", bufs=1))
+
+        a0 = keep.tile([P, CHUNKS, NODES], BF16)
+        for c in range(CHUNKS):
+            nc.sync.dma_start(out=a0[:, c, :], in_=inp[c * P : (c + 1) * P, FEATS : FEATS + NODES])
+        w_rows = keep.tile([P, PACK, DOUT], BF16)
+        nc.sync.dma_start(
+            out=w_rows[:].rearrange("p (u e) o -> p u (e o)", u=2),
+            in_=weight.rearrange("(u p e) o -> p u (e o)", u=2, e=2),
+        )
+        x = keep.tile([P, CHUNKS, FEATS], BF16)
+        for h in range(2):
+            nc.sync.dma_start(
+                out=x[:, 2 * h : 2 * h + 2, :],
+                in_=inp[2 * h * P : (2 * h + 2) * P, 0:FEATS].rearrange("(c p) k -> p c k", p=P),
+            )
+
+        ident = keep.tile([P, P], F32)
+        make_identity(nc, ident[:])
+        eye_wide = keep.tile([P, 2 * NODES - P], BF16)
+        nc.vector.memset(eye_wide[:], 0.0)
+        nc.vector.tensor_copy(out=eye_wide[:, NODES - P : NODES], in_=ident[:])
+        ones = keep.tile([P, 1], BF16)
+        nc.vector.memset(ones[:], 1.0)
+        warm = keep.tile([P, 1], F32)
+        nc.scalar.activation(out=warm[:], in_=ones[:], func=ACT.Sqrt)
+
+        colsum = psum.tile([P, CHUNKS], F32)
+        for c in range(CHUNKS):
+            for t in range(CHUNKS):
+                nc.tensor.matmul(
+                    out=colsum[:, t : t + 1],
+                    lhsT=a0[:, c, t * P : (t + 1) * P],
+                    rhs=ones[:],
+                    start=(c == 0 and t == 0),
+                    stop=(c == CHUNKS - 1 and t == CHUNKS - 1),
+                )
+
+        a_f32 = keep.tile([P, CHUNKS, NODES], F32)
+        for c in range(CHUNKS):
+            first = (CHUNKS - 1 - c) * P
+            nc.vector.tensor_tensor(
+                out=a_f32[:, c, :], in0=a0[:, c, :], in1=eye_wide[:, first : first + NODES], op=ALU.add
+            )
+            nc.sync.dma_start(out=out[c * P : (c + 1) * P, DOUT : DOUT + NODES], in_=a_f32[:, c, :])
+
+        root = keep.tile([P, CHUNKS], F32)
+        nc.scalar.activation(out=root[:], in_=colsum[:], func=ACT.Sqrt, bias=1.0)
+        r = keep.tile([P, CHUNKS], F32)
+        nc.vector.reciprocal(out=r[:], in_=root[:])
+
+        w_grouped = keep.tile([P, DOUT, PACK], BF16, align_bytes=64)
+        nc.scalar.copy(out=w_grouped[:], in_=w_rows[:].rearrange("p t o -> p o t"))
+        w_codes = keep.tile([P, DOUT], U32, align_bytes=64)
+        w_scales = keep.tile([P, DOUT], U8, align_bytes=64)
+        nc.vector.quantize_mx(
+            out=w_codes[:].bitcast(FP8X4),
+            scales=w_scales[:],
+            in_=w_grouped[:].rearrange("p o t -> p (o t)"),
+        )
+
+        x_grouped = keep.tile([P, NODES, PACK], BF16, align_bytes=64)
+        x_codes = keep.tile([P, NODES], U32, align_bytes=64)
+        x_scales = keep.tile([P, NODES], U8, align_bytes=64)
+        for h in range(2):
+            xt = psum.tile([P, 2, 2, P], F32, name="xt%d" % h)
+            for cc in range(2):
+                x_words = x[:, 2 * h + cc, :].bitcast(F32)
+                for u in range(2):
+                    nc.tensor.transpose(xt[:, cc, u, :], x_words[:, u * P : (u + 1) * P], ident[:])
+            half = slice(2 * h * P, (2 * h + 2) * P)
+            nc.scalar.copy(
+                out=x_grouped[:, half, :].bitcast(F32).rearrange("p (cc n) u -> p cc n u", cc=2),
+                in_=xt[:].rearrange("p cc u n -> p cc n u"),
+            )
+            nc.vector.quantize_mx(
+                out=x_codes[:, half].bitcast(FP8X4),
+                scales=x_scales[:, half],
+                in_=x_grouped[:, half, :].rearrange("p n t -> p (n t)"),
+            )
+
+        support = psum.tile([P, CHUNKS, DOUT], F32)
+        for c in range(CHUNKS):
+            nodes = slice(c * P, (c + 1) * P)
+            nc.tensor.matmul_mx(
+                out=support[:, c, :],
+                lhsT=x_codes[:, nodes].bitcast(FP8X4),
+                lhsT_scale=x_scales[:, nodes],
+                rhs=w_codes[:].bitcast(FP8X4),
+                rhs_scale=w_scales[:],
+                start=True,
+                stop=True,
+            )
+        s_grouped = keep.tile([P, DOUT, PACK], BF16, align_bytes=64)
+        nc.scalar.copy(out=s_grouped[:], in_=support[:].rearrange("p t o -> p o t"))
+        s_codes = keep.tile([P, DOUT], U32, align_bytes=64)
+        s_scales = keep.tile([P, DOUT], U8, align_bytes=64)
+        nc.vector.quantize_mx(
+            out=s_codes[:].bitcast(FP8X4),
+            scales=s_scales[:],
+            in_=s_grouped[:].rearrange("p o t -> p (o t)"),
+        )
+
+        dad_grouped = keep.tile([P, NODES, PACK], BF16, align_bytes=64)
+        dad_codes = keep.tile([P, NODES], U32, align_bytes=64)
+        dad_scales = keep.tile([P, NODES], U8, align_bytes=64)
+        product = psum.tile([P, CHUNKS, DOUT], F32)
+        result = keep.tile([P, CHUNKS, DOUT], F32)
+        for c in range(CHUNKS):
+            rows = slice(c * P, (c + 1) * P)
+            row_scaled = keep.tile([P, NODES], F32, name="row_scaled%d" % c)
+            if c % 2 == 0:
+                nc.vector.tensor_scalar(
+                    out=row_scaled[:], in0=a_f32[:, c, :], scalar1=r[:, c : c + 1], scalar2=None, op0=ALU.mult
+                )
+            else:
+                nc.scalar.activation(out=row_scaled[:], in_=a_f32[:, c, :], func=ACT.Copy, scale=r[:, c : c + 1])
+            flipped = psum.tile([P, PACK, P], F32, tag="flipped", bufs=3)
+            for t in range(PACK):
+                nc.tensor.transpose(flipped[:, t, :], row_scaled[:, t * P : (t + 1) * P], ident[:])
+            nc.vector.tensor_tensor(
+                out=dad_grouped[:, rows, :],
+                in0=flipped[:].rearrange("p t i -> p i t"),
+                in1=r[:].unsqueeze(1).to_broadcast([P, P, PACK]),
+                op=ALU.mult,
+            )
+            nc.vector.quantize_mx(
+                out=dad_codes[:, rows].bitcast(FP8X4),
+                scales=dad_scales[:, rows],
+                in_=dad_grouped[:, rows, :].rearrange("p i t -> p (i t)"),
+            )
+            nc.tensor.matmul_mx(
+                out=product[:, c, :],
+                lhsT=dad_codes[:, rows].bitcast(FP8X4),
+                lhsT_scale=dad_scales[:, rows],
+                rhs=s_codes[:].bitcast(FP8X4),
+                rhs_scale=s_scales[:],
+                start=True,
+                stop=True,
+            )
+            nc.scalar.copy(out=result[:, c, :], in_=product[:, c, :])
+            nc.sync.dma_start(out=out[rows, 0:DOUT], in_=result[:, c, :])

@@ -17,6 +17,8 @@ NODES = 512
 FEATS = 512
 DOUT = 128
 CHUNKS = NODES // P
+HALF = NODES // 2
+HALVES = 2
 
 FLOPS = 2 * NODES * FEATS * DOUT + 2 * NODES * NODES * DOUT
 
@@ -25,7 +27,8 @@ def tile_crossviewgcn_layer1_s_kernel(tc, inp, weight, out):
     nc = tc.nc
     with ExitStack() as ctx:
         keep = ctx.enter_context(tc.tile_pool(name="keep", bufs=1))
-        psum = ctx.enter_context(tc.psum_pool(name="psum", bufs=1))
+        psum = ctx.enter_context(tc.psum_pool(name="psum", bufs=8))
+        ctx.enter_context(tc.manual_schedule())
 
         a0 = keep.tile([P, CHUNKS, NODES], BF16)
         for c in range(CHUNKS):
@@ -36,23 +39,24 @@ def tile_crossviewgcn_layer1_s_kernel(tc, inp, weight, out):
             in_=weight.rearrange("(u p e) o -> p u (e o)", u=2, e=2),
         )
         x = keep.tile([P, CHUNKS, FEATS], BF16)
-        for h in range(2):
+        for h in range(HALVES):
             nc.sync.dma_start(
                 out=x[:, 2 * h : 2 * h + 2, :],
-                in_=inp[2 * h * P : (2 * h + 2) * P, 0:FEATS].rearrange("(c p) k -> p c k", p=P),
+                in_=inp[h * HALF : (h + 1) * HALF, 0:FEATS].rearrange("(c p) k -> p c k", p=P),
             )
 
         ident = keep.tile([P, P], F32)
         make_identity(nc, ident[:])
-        eye_wide = keep.tile([P, 2 * NODES - P], BF16)
+        eye_wide = keep.tile([P, 3 * P], BF16)
         nc.vector.memset(eye_wide[:], 0.0)
-        nc.vector.tensor_copy(out=eye_wide[:, NODES - P : NODES], in_=ident[:])
+        nc.vector.tensor_copy(out=eye_wide[:, P : 2 * P], in_=ident[:])
         ones = keep.tile([P, 1], BF16)
         nc.vector.memset(ones[:], 1.0)
         warm = keep.tile([P, 1], F32)
         nc.scalar.activation(out=warm[:], in_=ones[:], func=ACT.Sqrt)
 
-        colsum = psum.tile([P, CHUNKS], F32)
+        colsum = psum.tile([P, CHUNKS], F32, tag="bank")
+        a_f32 = keep.tile([P, CHUNKS, NODES], F32)
         for c in range(CHUNKS):
             for t in range(CHUNKS):
                 nc.tensor.matmul(
@@ -62,13 +66,13 @@ def tile_crossviewgcn_layer1_s_kernel(tc, inp, weight, out):
                     start=(c == 0 and t == 0),
                     stop=(c == CHUNKS - 1 and t == CHUNKS - 1),
                 )
-
-        a_f32 = keep.tile([P, CHUNKS, NODES], F32)
-        for c in range(CHUNKS):
-            first = (CHUNKS - 1 - c) * P
+            with_diag = slice((c // 2) * HALF, (c // 2 + 1) * HALF)
+            without = slice((1 - c // 2) * HALF, (2 - c // 2) * HALF)
+            first = (1 - c % 2) * P
             nc.vector.tensor_tensor(
-                out=a_f32[:, c, :], in0=a0[:, c, :], in1=eye_wide[:, first : first + NODES], op=ALU.add
+                out=a_f32[:, c, with_diag], in0=a0[:, c, with_diag], in1=eye_wide[:, first : first + HALF], op=ALU.add
             )
+            nc.scalar.copy(out=a_f32[:, c, without], in_=a0[:, c, without])
             nc.sync.dma_start(out=out[c * P : (c + 1) * P, DOUT : DOUT + NODES], in_=a_f32[:, c, :])
 
         root = keep.tile([P, CHUNKS], F32)
@@ -77,36 +81,87 @@ def tile_crossviewgcn_layer1_s_kernel(tc, inp, weight, out):
         nc.vector.reciprocal(out=r[:], in_=root[:])
 
         w_grouped = keep.tile([P, DOUT, PACK], BF16, align_bytes=64)
-        nc.scalar.copy(out=w_grouped[:], in_=w_rows[:].rearrange("p t o -> p o t"))
         w_codes = keep.tile([P, DOUT], U32, align_bytes=64)
         w_scales = keep.tile([P, DOUT], U8, align_bytes=64)
-        nc.vector.quantize_mx(
-            out=w_codes[:].bitcast(FP8X4),
-            scales=w_scales[:],
-            in_=w_grouped[:].rearrange("p o t -> p (o t)"),
-        )
-
         x_grouped = keep.tile([P, NODES, PACK], BF16, align_bytes=64)
         x_codes = keep.tile([P, NODES], U32, align_bytes=64)
         x_scales = keep.tile([P, NODES], U8, align_bytes=64)
-        for h in range(2):
-            xt = psum.tile([P, 2, 2, P], F32, name="xt%d" % h)
+        s_grouped = keep.tile([P, DOUT, PACK], BF16, align_bytes=64)
+        s_codes = keep.tile([P, DOUT], U32, align_bytes=64)
+        s_scales = keep.tile([P, DOUT], U8, align_bytes=64)
+        dad_grouped = keep.tile([P, NODES, PACK], BF16, align_bytes=64)
+        dad_codes = keep.tile([P, NODES], U32, align_bytes=64)
+        dad_scales = keep.tile([P, NODES], U8, align_bytes=64)
+        row_scaled = keep.tile([P, CHUNKS, NODES], F32)
+        result = keep.tile([P, CHUNKS, DOUT], F32)
+        x_flipped = {}
+        flipped = {}
+
+        def scale_rows(engine_is_vector, c):
+            if engine_is_vector:
+                nc.vector.tensor_scalar(
+                    out=row_scaled[:, c, :], in0=a_f32[:, c, :], scalar1=r[:, c : c + 1], scalar2=None, op0=ALU.mult
+                )
+            else:
+                nc.scalar.activation(out=row_scaled[:, c, :], in_=a_f32[:, c, :], func=ACT.Copy, scale=r[:, c : c + 1])
+
+        def transpose_rows(c):
+            flipped[c] = psum.tile([P, PACK, P], F32, tag="bank", name="flipped%d" % c)
+            for t in range(PACK):
+                nc.tensor.transpose(flipped[c][:, t, :], row_scaled[:, c, t * P : (t + 1) * P], ident[:])
+
+        def scale_columns(c):
+            nc.vector.tensor_tensor(
+                out=dad_grouped[:, c * P : (c + 1) * P, :],
+                in0=flipped[c][:].rearrange("p t i -> p i t"),
+                in1=r[:].unsqueeze(1).to_broadcast([P, P, PACK]),
+                op=ALU.mult,
+            )
+
+        def quantise(codes, scales, grouped):
+            nc.vector.quantize_mx(
+                out=codes.bitcast(FP8X4), scales=scales, in_=grouped.rearrange("p w t -> p (w t)")
+            )
+
+        def quantise_dad(c):
+            rows = slice(c * P, (c + 1) * P)
+            quantise(dad_codes[:, rows], dad_scales[:, rows], dad_grouped[:, rows, :])
+
+        def transpose_x(h):
+            x_flipped[h] = psum.tile([P, 2, 2, P], F32, tag="bank", name="x_flipped%d" % h)
             for cc in range(2):
                 x_words = x[:, 2 * h + cc, :].bitcast(F32)
                 for u in range(2):
-                    nc.tensor.transpose(xt[:, cc, u, :], x_words[:, u * P : (u + 1) * P], ident[:])
-            half = slice(2 * h * P, (2 * h + 2) * P)
+                    nc.tensor.transpose(x_flipped[h][:, cc, u, :], x_words[:, u * P : (u + 1) * P], ident[:])
+
+        def copy_x(h):
             nc.scalar.copy(
-                out=x_grouped[:, half, :].bitcast(F32).rearrange("p (cc n) u -> p cc n u", cc=2),
-                in_=xt[:].rearrange("p cc u n -> p cc n u"),
-            )
-            nc.vector.quantize_mx(
-                out=x_codes[:, half].bitcast(FP8X4),
-                scales=x_scales[:, half],
-                in_=x_grouped[:, half, :].rearrange("p n t -> p (n t)"),
+                out=x_grouped[:, h * HALF : (h + 1) * HALF, :].bitcast(F32).rearrange("p (cc n) u -> p cc n u", cc=2),
+                in_=x_flipped[h][:].rearrange("p cc u n -> p cc n u"),
             )
 
-        support = psum.tile([P, CHUNKS, DOUT], F32)
+        def quantise_x(h):
+            nodes = slice(h * HALF, (h + 1) * HALF)
+            quantise(x_codes[:, nodes], x_scales[:, nodes], x_grouped[:, nodes, :])
+
+        scale_rows(True, 0)
+        nc.vector.tensor_copy(out=w_grouped[:], in_=w_rows[:].rearrange("p t o -> p o t"))
+        quantise(w_codes[:], w_scales[:], w_grouped[:])
+        for c in range(CHUNKS):
+            if c < HALVES:
+                transpose_x(c)
+            transpose_rows(c)
+            if c + 1 < CHUNKS:
+                scale_rows(False, c + 1)
+            if c < HALVES:
+                copy_x(c)
+            scale_columns(c)
+            if c >= 1:
+                quantise_dad(c - 1)
+            if c < HALVES:
+                quantise_x(c)
+
+        support = psum.tile([P, CHUNKS, DOUT], F32, tag="bank")
         for c in range(CHUNKS):
             nodes = slice(c * P, (c + 1) * P)
             nc.tensor.matmul_mx(
@@ -118,46 +173,15 @@ def tile_crossviewgcn_layer1_s_kernel(tc, inp, weight, out):
                 start=True,
                 stop=True,
             )
-        s_grouped = keep.tile([P, DOUT, PACK], BF16, align_bytes=64)
         nc.scalar.copy(out=s_grouped[:], in_=support[:].rearrange("p t o -> p o t"))
-        s_codes = keep.tile([P, DOUT], U32, align_bytes=64)
-        s_scales = keep.tile([P, DOUT], U8, align_bytes=64)
-        nc.vector.quantize_mx(
-            out=s_codes[:].bitcast(FP8X4),
-            scales=s_scales[:],
-            in_=s_grouped[:].rearrange("p o t -> p (o t)"),
-        )
+        quantise(s_codes[:], s_scales[:], s_grouped[:])
+        quantise_dad(CHUNKS - 1)
 
-        dad_grouped = keep.tile([P, NODES, PACK], BF16, align_bytes=64)
-        dad_codes = keep.tile([P, NODES], U32, align_bytes=64)
-        dad_scales = keep.tile([P, NODES], U8, align_bytes=64)
-        product = psum.tile([P, CHUNKS, DOUT], F32)
-        result = keep.tile([P, CHUNKS, DOUT], F32)
         for c in range(CHUNKS):
             rows = slice(c * P, (c + 1) * P)
-            row_scaled = keep.tile([P, NODES], F32, name="row_scaled%d" % c)
-            if c % 2 == 0:
-                nc.vector.tensor_scalar(
-                    out=row_scaled[:], in0=a_f32[:, c, :], scalar1=r[:, c : c + 1], scalar2=None, op0=ALU.mult
-                )
-            else:
-                nc.scalar.activation(out=row_scaled[:], in_=a_f32[:, c, :], func=ACT.Copy, scale=r[:, c : c + 1])
-            flipped = psum.tile([P, PACK, P], F32, tag="flipped", bufs=3)
-            for t in range(PACK):
-                nc.tensor.transpose(flipped[:, t, :], row_scaled[:, t * P : (t + 1) * P], ident[:])
-            nc.vector.tensor_tensor(
-                out=dad_grouped[:, rows, :],
-                in0=flipped[:].rearrange("p t i -> p i t"),
-                in1=r[:].unsqueeze(1).to_broadcast([P, P, PACK]),
-                op=ALU.mult,
-            )
-            nc.vector.quantize_mx(
-                out=dad_codes[:, rows].bitcast(FP8X4),
-                scales=dad_scales[:, rows],
-                in_=dad_grouped[:, rows, :].rearrange("p i t -> p (i t)"),
-            )
+            product = psum.tile([P, DOUT], F32, tag="bank", name="product%d" % c)
             nc.tensor.matmul_mx(
-                out=product[:, c, :],
+                out=product[:],
                 lhsT=dad_codes[:, rows].bitcast(FP8X4),
                 lhsT_scale=dad_scales[:, rows],
                 rhs=s_codes[:].bitcast(FP8X4),
@@ -165,5 +189,8 @@ def tile_crossviewgcn_layer1_s_kernel(tc, inp, weight, out):
                 start=True,
                 stop=True,
             )
-            nc.scalar.copy(out=result[:, c, :], in_=product[:, c, :])
+            if c == CHUNKS - 1:
+                nc.vector.tensor_copy(out=result[:, c, :], in_=product[:])
+            else:
+                nc.scalar.copy(out=result[:, c, :], in_=product[:])
             nc.sync.dma_start(out=out[rows, 0:DOUT], in_=result[:, c, :])

@@ -53,7 +53,7 @@ def tile_crossviewgcn_layer1_s_kernel(tc, inp, weight, out):
         ones = keep.tile([P, 1], BF16)
         nc.vector.memset(ones[:], 1.0)
         warm = keep.tile([P, 1], F32)
-        nc.scalar.activation(out=warm[:], in_=ones[:], func=ACT.Sqrt)
+        nc.scalar.activation(out=warm[:], in_=ones[:], func=ACT.Abs_reciprocal_sqrt)
 
         colsum = psum.tile([P, CHUNKS], F32, tag="bank")
         a_f32 = keep.tile([P, CHUNKS, NODES], F32)
@@ -75,10 +75,8 @@ def tile_crossviewgcn_layer1_s_kernel(tc, inp, weight, out):
             nc.scalar.copy(out=a_f32[:, c, without], in_=a0[:, c, without])
             nc.sync.dma_start(out=out[c * P : (c + 1) * P, DOUT : DOUT + NODES], in_=a_f32[:, c, :])
 
-        root = keep.tile([P, CHUNKS], F32)
-        nc.scalar.activation(out=root[:], in_=colsum[:], func=ACT.Sqrt, bias=1.0)
         r = keep.tile([P, CHUNKS], F32)
-        nc.vector.reciprocal(out=r[:], in_=root[:])
+        nc.scalar.activation(out=r[:], in_=colsum[:], func=ACT.Abs_reciprocal_sqrt, bias=1.0)
 
         w_grouped = keep.tile([P, DOUT, PACK], BF16, align_bytes=64)
         w_codes = keep.tile([P, DOUT], U32, align_bytes=64)

@@ -33,17 +33,14 @@ def tile_crossviewgcn_layer1_s_kernel(tc, inp, weight, out):
         a0 = keep.tile([P, CHUNKS, NODES], BF16)
         for c in range(CHUNKS):
             nc.sync.dma_start(out=a0[:, c, :], in_=inp[c * P : (c + 1) * P, FEATS : FEATS + NODES])
+        x = keep.tile([P, CHUNKS, FEATS], BF16)
+        for c in range(CHUNKS):
+            nc.sync.dma_start(out=x[:, c, :], in_=inp[c * P : (c + 1) * P, 0:FEATS])
         w_rows = keep.tile([P, PACK, DOUT], BF16)
         nc.sync.dma_start(
             out=w_rows[:].rearrange("p (u e) o -> p u (e o)", u=2),
             in_=weight.rearrange("(u p e) o -> p u (e o)", u=2, e=2),
         )
-        x = keep.tile([P, CHUNKS, FEATS], BF16)
-        for h in range(HALVES):
-            nc.sync.dma_start(
-                out=x[:, 2 * h : 2 * h + 2, :],
-                in_=inp[h * HALF : (h + 1) * HALF, 0:FEATS].rearrange("(c p) k -> p c k", p=P),
-            )
 
         ident = keep.tile([P, P], F32)
         make_identity(nc, ident[:])
@@ -92,72 +89,44 @@ def tile_crossviewgcn_layer1_s_kernel(tc, inp, weight, out):
         dad_scales = keep.tile([P, NODES], U8, align_bytes=64)
         row_scaled = keep.tile([P, CHUNKS, NODES], F32)
         result = keep.tile([P, CHUNKS, DOUT], F32)
-        x_flipped = {}
-        flipped = {}
-
-        def scale_rows(engine_is_vector, c):
-            if engine_is_vector:
-                nc.vector.tensor_scalar(
-                    out=row_scaled[:, c, :], in0=a_f32[:, c, :], scalar1=r[:, c : c + 1], scalar2=None, op0=ALU.mult
-                )
-            else:
-                nc.scalar.activation(out=row_scaled[:, c, :], in_=a_f32[:, c, :], func=ACT.Copy, scale=r[:, c : c + 1])
-
-        def transpose_rows(c):
-            flipped[c] = psum.tile([P, PACK, P], F32, tag="bank", name="flipped%d" % c)
-            for t in range(PACK):
-                nc.tensor.transpose(flipped[c][:, t, :], row_scaled[:, c, t * P : (t + 1) * P], ident[:])
-
-        def scale_columns(c):
-            nc.vector.tensor_tensor(
-                out=dad_grouped[:, c * P : (c + 1) * P, :],
-                in0=flipped[c][:].rearrange("p t i -> p i t"),
-                in1=r[:].unsqueeze(1).to_broadcast([P, P, PACK]),
-                op=ALU.mult,
-            )
 
         def quantise(codes, scales, grouped):
             nc.vector.quantize_mx(
                 out=codes.bitcast(FP8X4), scales=scales, in_=grouped.rearrange("p w t -> p (w t)")
             )
 
-        def quantise_dad(c):
-            rows = slice(c * P, (c + 1) * P)
-            quantise(dad_codes[:, rows], dad_scales[:, rows], dad_grouped[:, rows, :])
-
-        def transpose_x(h):
-            x_flipped[h] = psum.tile([P, 2, 2, P], F32, tag="bank", name="x_flipped%d" % h)
-            for cc in range(2):
-                x_words = x[:, 2 * h + cc, :].bitcast(F32)
-                for u in range(2):
-                    nc.tensor.transpose(x_flipped[h][:, cc, u, :], x_words[:, u * P : (u + 1) * P], ident[:])
-
-        def copy_x(h):
+        for c in range(CHUNKS):
+            x_flipped = psum.tile([P, 2, P], F32, tag="bank")
+            x_words = x[:, c, :].bitcast(F32)
+            for u in range(2):
+                nc.tensor.transpose(x_flipped[:, u, :], x_words[:, u * P : (u + 1) * P], ident[:])
             nc.scalar.copy(
-                out=x_grouped[:, h * HALF : (h + 1) * HALF, :].bitcast(F32).rearrange("p (cc n) u -> p cc n u", cc=2),
-                in_=x_flipped[h][:].rearrange("p cc u n -> p cc n u"),
+                out=x_grouped[:, c * P : (c + 1) * P, :].bitcast(F32), in_=x_flipped[:].rearrange("p u n -> p n u")
             )
+        nc.scalar.copy(out=w_grouped[:], in_=w_rows[:].rearrange("p t o -> p o t"))
 
-        def quantise_x(h):
-            nodes = slice(h * HALF, (h + 1) * HALF)
-            quantise(x_codes[:, nodes], x_scales[:, nodes], x_grouped[:, nodes, :])
+        for c in range(CHUNKS):
+            nc.vector.tensor_scalar(
+                out=row_scaled[:, c, :], in0=a_f32[:, c, :], scalar1=r[:, c : c + 1], scalar2=None, op0=ALU.mult
+            )
+        flipped = []
+        for c in range(CHUNKS):
+            flipped.append(psum.tile([P, PACK, P], F32, tag="bank", name="flipped%d" % c))
+            for t in range(PACK):
+                nc.tensor.transpose(flipped[c][:, t, :], row_scaled[:, c, t * P : (t + 1) * P], ident[:])
 
-        scale_rows(True, 0)
-        nc.vector.tensor_copy(out=w_grouped[:], in_=w_rows[:].rearrange("p t o -> p o t"))
-        quantise(w_codes[:], w_scales[:], w_grouped[:])
         for c in range(CHUNKS):
             if c < HALVES:
-                transpose_x(c)
-            transpose_rows(c)
-            if c + 1 < CHUNKS:
-                scale_rows(False, c + 1)
-            if c < HALVES:
-                copy_x(c)
-            scale_columns(c)
-            if c >= 1:
-                quantise_dad(c - 1)
-            if c < HALVES:
-                quantise_x(c)
+                nodes = slice(c * HALF, (c + 1) * HALF)
+                quantise(x_codes[:, nodes], x_scales[:, nodes], x_grouped[:, nodes, :])
+            if c == HALVES - 1:
+                quantise(w_codes[:], w_scales[:], w_grouped[:])
+            nc.vector.tensor_tensor(
+                out=dad_grouped[:, c * P : (c + 1) * P, :],
+                in0=flipped[c][:].rearrange("p t i -> p i t"),
+                in1=r[:].unsqueeze(1).to_broadcast([P, P, PACK]),
+                op=ALU.mult,
+            )
 
         support = psum.tile([P, CHUNKS, DOUT], F32, tag="bank")
         for c in range(CHUNKS):
@@ -172,12 +141,15 @@ def tile_crossviewgcn_layer1_s_kernel(tc, inp, weight, out):
                 stop=True,
             )
         nc.scalar.copy(out=s_grouped[:], in_=support[:].rearrange("p t o -> p o t"))
-        quantise(s_codes[:], s_scales[:], s_grouped[:])
-        quantise_dad(CHUNKS - 1)
 
         for c in range(CHUNKS):
             rows = slice(c * P, (c + 1) * P)
-            product = psum.tile([P, DOUT], F32, tag="bank", name="product%d" % c)
+            quantise(dad_codes[:, rows], dad_scales[:, rows], dad_grouped[:, rows, :])
+        quantise(s_codes[:], s_scales[:], s_grouped[:])
+
+        for c in range(CHUNKS):
+            rows = slice(c * P, (c + 1) * P)
+            product = psum.tile([P, DOUT], F32, tag="bank")
             nc.tensor.matmul_mx(
                 out=product[:],
                 lhsT=dad_codes[:, rows].bitcast(FP8X4),

@@ -34,8 +34,11 @@ def tile_crossviewgcn_layer1_s_kernel(tc, inp, weight, out):
         for c in range(CHUNKS):
             nc.sync.dma_start(out=a0[:, c, :], in_=inp[c * P : (c + 1) * P, FEATS : FEATS + NODES])
         x = keep.tile([P, CHUNKS, FEATS], BF16)
-        for c in range(CHUNKS):
-            nc.sync.dma_start(out=x[:, c, :], in_=inp[c * P : (c + 1) * P, 0:FEATS])
+        for u in range(HALVES):
+            nc.sync.dma_start(
+                out=x[:, 2 * u : 2 * u + 2, :],
+                in_=inp[u * HALF : (u + 1) * HALF, 0:FEATS].rearrange("(p e) k -> p e k", e=2),
+            )
         w_rows = keep.tile([P, PACK, DOUT], BF16)
         nc.sync.dma_start(
             out=w_rows[:].rearrange("p (u e) o -> p u (e o)", u=2),
@@ -84,10 +87,10 @@ def tile_crossviewgcn_layer1_s_kernel(tc, inp, weight, out):
         s_grouped = keep.tile([P, DOUT, PACK], BF16, align_bytes=64)
         s_codes = keep.tile([P, DOUT], U32, align_bytes=64)
         s_scales = keep.tile([P, DOUT], U8, align_bytes=64)
+        dad = keep.tile([P, CHUNKS, NODES], BF16, align_bytes=64)
         dad_grouped = keep.tile([P, NODES, PACK], BF16, align_bytes=64)
         dad_codes = keep.tile([P, NODES], U32, align_bytes=64)
         dad_scales = keep.tile([P, NODES], U8, align_bytes=64)
-        row_scaled = keep.tile([P, CHUNKS, NODES], F32)
         result = keep.tile([P, CHUNKS, DOUT], F32)
 
         def quantise(codes, scales, grouped):
@@ -95,38 +98,56 @@ def tile_crossviewgcn_layer1_s_kernel(tc, inp, weight, out):
                 out=codes.bitcast(FP8X4), scales=scales, in_=grouped.rearrange("p w t -> p (w t)")
             )
 
-        for c in range(CHUNKS):
-            x_flipped = psum.tile([P, 2, P], F32, tag="bank")
-            x_words = x[:, c, :].bitcast(F32)
+        def turn(rows, name):
+            flipped = psum.tile([P, 2, P], F32, tag="bank", name=name)
+            words = rows.bitcast(F32)
             for u in range(2):
-                nc.tensor.transpose(x_flipped[:, u, :], x_words[:, u * P : (u + 1) * P], ident[:])
+                nc.tensor.transpose(flipped[:, u, :], words[:, u * P : (u + 1) * P], ident[:])
+            return flipped
+
+        def group(grouped, c, flipped):
             nc.scalar.copy(
-                out=x_grouped[:, c * P : (c + 1) * P, :].bitcast(F32), in_=x_flipped[:].rearrange("p u n -> p n u")
+                out=grouped[:, c * P : (c + 1) * P, :].bitcast(F32), in_=flipped[:].rearrange("p u n -> p n u")
             )
+
+        def scale(c):
+            nc.vector.scalar_tensor_tensor(
+                out=dad[:, c, :], in0=a_f32[:, c, :], scalar=r[:, c : c + 1], in1=r_row[:], op0=ALU.mult, op1=ALU.mult
+            )
+
+        def quantise_x(h):
+            nodes = slice(h * HALF, (h + 1) * HALF)
+            quantise(x_codes[:, nodes], x_scales[:, nodes], x_grouped[:, nodes, :])
+
+        def quantise_dad(c):
+            rows = slice(c * P, (c + 1) * P)
+            quantise(dad_codes[:, rows], dad_scales[:, rows], dad_grouped[:, rows, :])
+
+        x_turned = [turn(x[:, 0, :], "x0")]
+        r_row = psum.tile([P, NODES], F32, tag="bank")
+        for t in range(CHUNKS):
+            nc.tensor.transpose(r_row[:, t * P : (t + 1) * P], r[:, t : t + 1].to_broadcast([P, P]), ident[:])
+        for t in range(1, CHUNKS):
+            x_turned.append(turn(x[:, t, :], "x%d" % t))
+
+        scale(0)
+        dad_turned = [turn(dad[:, 0, :], "d0")]
+        group(x_grouped, 0, x_turned[0])
+        group(x_grouped, 1, x_turned[1])
+        scale(1)
+        dad_turned.append(turn(dad[:, 1, :], "d1"))
+        group(x_grouped, 2, x_turned[2])
+        group(x_grouped, 3, x_turned[3])
+        quantise_x(0)
+        scale(2)
         nc.scalar.copy(out=w_grouped[:], in_=w_rows[:].rearrange("p t o -> p o t"))
-
-        for c in range(CHUNKS):
-            nc.vector.tensor_scalar(
-                out=row_scaled[:, c, :], in0=a_f32[:, c, :], scalar1=r[:, c : c + 1], scalar2=None, op0=ALU.mult
-            )
-        flipped = []
-        for c in range(CHUNKS):
-            flipped.append(psum.tile([P, PACK, P], F32, tag="bank", name="flipped%d" % c))
-            for t in range(PACK):
-                nc.tensor.transpose(flipped[c][:, t, :], row_scaled[:, c, t * P : (t + 1) * P], ident[:])
-
-        for c in range(CHUNKS):
-            if c < HALVES:
-                nodes = slice(c * HALF, (c + 1) * HALF)
-                quantise(x_codes[:, nodes], x_scales[:, nodes], x_grouped[:, nodes, :])
-            if c == HALVES - 1:
-                quantise(w_codes[:], w_scales[:], w_grouped[:])
-            nc.vector.tensor_tensor(
-                out=dad_grouped[:, c * P : (c + 1) * P, :],
-                in0=flipped[c][:].rearrange("p t i -> p i t"),
-                in1=r[:].unsqueeze(1).to_broadcast([P, P, PACK]),
-                op=ALU.mult,
-            )
+        group(dad_grouped, 0, dad_turned[0])
+        group(dad_grouped, 1, dad_turned[1])
+        quantise_x(1)
+        quantise(w_codes[:], w_scales[:], w_grouped[:])
+        dad_turned.append(turn(dad[:, 2, :], "d2"))
+        group(dad_grouped, 2, dad_turned[2])
+        scale(3)
 
         support = psum.tile([P, CHUNKS, DOUT], F32, tag="bank")
         for c in range(CHUNKS):
@@ -140,12 +161,14 @@ def tile_crossviewgcn_layer1_s_kernel(tc, inp, weight, out):
                 start=True,
                 stop=True,
             )
+        dad_turned.append(turn(dad[:, 3, :], "d3"))
         nc.scalar.copy(out=s_grouped[:], in_=support[:].rearrange("p t o -> p o t"))
-
-        for c in range(CHUNKS):
-            rows = slice(c * P, (c + 1) * P)
-            quantise(dad_codes[:, rows], dad_scales[:, rows], dad_grouped[:, rows, :])
+        group(dad_grouped, 3, dad_turned[3])
+        quantise_dad(0)
+        quantise_dad(1)
+        quantise_dad(2)
         quantise(s_codes[:], s_scales[:], s_grouped[:])
+        quantise_dad(3)
 
         for c in range(CHUNKS):
             rows = slice(c * P, (c + 1) * P)

@@ -34,11 +34,8 @@ def tile_crossviewgcn_layer1_s_kernel(tc, inp, weight, out):
         for c in range(CHUNKS):
             nc.sync.dma_start(out=a0[:, c, :], in_=inp[c * P : (c + 1) * P, FEATS : FEATS + NODES])
         x = keep.tile([P, CHUNKS, FEATS], BF16)
-        for u in range(HALVES):
-            nc.sync.dma_start(
-                out=x[:, 2 * u : 2 * u + 2, :],
-                in_=inp[u * HALF : (u + 1) * HALF, 0:FEATS].rearrange("(p e) k -> p e k", e=2),
-            )
+        for c in range(CHUNKS):
+            nc.sync.dma_start(out=x[:, c, :], in_=inp[c * P : (c + 1) * P, 0:FEATS])
         w_rows = keep.tile([P, PACK, DOUT], BF16)
         nc.sync.dma_start(
             out=w_rows[:].rearrange("p (u e) o -> p u (e o)", u=2),
@@ -47,6 +44,9 @@ def tile_crossviewgcn_layer1_s_kernel(tc, inp, weight, out):
 
         ident = keep.tile([P, P], F32)
         make_identity(nc, ident[:])
+        warm_bank = psum.tile([P, P], F32, tag="bank")
+        for i in range(3):
+            nc.tensor.matmul(out=warm_bank[:], lhsT=ident[:], rhs=ident[:], start=True, stop=True)
         eye_wide = keep.tile([P, 3 * P], BF16)
         nc.vector.memset(eye_wide[:], 0.0)
         nc.vector.tensor_copy(out=eye_wide[:, P : 2 * P], in_=ident[:])
@@ -91,6 +91,7 @@ def tile_crossviewgcn_layer1_s_kernel(tc, inp, weight, out):
         dad_grouped = keep.tile([P, NODES, PACK], BF16, align_bytes=64)
         dad_codes = keep.tile([P, NODES], U32, align_bytes=64)
         dad_scales = keep.tile([P, NODES], U8, align_bytes=64)
+        row_scaled = keep.tile([P, 2, NODES], F32)
         result = keep.tile([P, CHUNKS, DOUT], F32)
 
         def quantise(codes, scales, grouped):
@@ -110,10 +111,36 @@ def tile_crossviewgcn_layer1_s_kernel(tc, inp, weight, out):
                 out=grouped[:, c * P : (c + 1) * P, :].bitcast(F32), in_=flipped[:].rearrange("p u n -> p n u")
             )
 
-        def scale(c):
-            nc.vector.scalar_tensor_tensor(
-                out=dad[:, c, :], in0=a_f32[:, c, :], scalar=r[:, c : c + 1], in1=r_row[:], op0=ALU.mult, op1=ALU.mult
+        def scale_rows(c):
+            nc.vector.tensor_scalar(
+                out=row_scaled[:, c, :], in0=a_f32[:, c, :], scalar1=r[:, c : c + 1], scalar2=None, op0=ALU.mult
             )
+
+        def turn_scaled(c):
+            flipped = psum.tile([P, PACK, P], F32, tag="bank", name="a%d" % c)
+            for t in range(PACK):
+                nc.tensor.transpose(flipped[:, t, :], row_scaled[:, c, t * P : (t + 1) * P], ident[:])
+            return flipped
+
+        def scale_columns(c, flipped):
+            nc.vector.tensor_tensor(
+                out=dad_grouped[:, c * P : (c + 1) * P, :],
+                in0=flipped[:].rearrange("p t i -> p i t"),
+                in1=r[:].unsqueeze(1).to_broadcast([P, P, PACK]),
+                op=ALU.mult,
+            )
+
+        def scale_both(c):
+            for u in range(2):
+                columns = slice(u * HALF, (u + 1) * HALF)
+                nc.vector.scalar_tensor_tensor(
+                    out=dad[:, c, columns].rearrange("p (k e) -> p k e", e=2),
+                    in0=a_f32[:, c, columns].rearrange("p (e k) -> p k e", e=2),
+                    scalar=r[:, c : c + 1],
+                    in1=r_row[:, columns].rearrange("p (e k) -> p k e", e=2),
+                    op0=ALU.mult,
+                    op1=ALU.mult,
+                )
 
         def quantise_x(h):
             nodes = slice(h * HALF, (h + 1) * HALF)
@@ -123,31 +150,35 @@ def tile_crossviewgcn_layer1_s_kernel(tc, inp, weight, out):
             rows = slice(c * P, (c + 1) * P)
             quantise(dad_codes[:, rows], dad_scales[:, rows], dad_grouped[:, rows, :])
 
-        x_turned = [turn(x[:, 0, :], "x0")]
+        scale_rows(0)
+        scale_rows(1)
         r_row = psum.tile([P, NODES], F32, tag="bank")
         for t in range(CHUNKS):
             nc.tensor.transpose(r_row[:, t * P : (t + 1) * P], r[:, t : t + 1].to_broadcast([P, P]), ident[:])
-        for t in range(1, CHUNKS):
-            x_turned.append(turn(x[:, t, :], "x%d" % t))
-
-        scale(0)
-        dad_turned = [turn(dad[:, 0, :], "d0")]
-        group(x_grouped, 0, x_turned[0])
-        group(x_grouped, 1, x_turned[1])
-        scale(1)
-        dad_turned.append(turn(dad[:, 1, :], "d1"))
-        group(x_grouped, 2, x_turned[2])
-        group(x_grouped, 3, x_turned[3])
+        x_turned = [turn(x[:, c, :], "x%d" % c) for c in range(CHUNKS)]
+        for c in range(CHUNKS):
+            group(x_grouped, c, x_turned[c])
+        nc.gpsimd.tensor_scalar(
+            out=w_grouped[:],
+            in0=w_rows[:].rearrange("p t o -> p o t"),
+            scalar1=1.0,
+            scalar2=0.0,
+            op0=ALU.mult,
+            op1=ALU.add,
+        )
+        a_turned = [turn_scaled(0)]
+        scale_both(2)
+        d2 = turn(dad[:, 2, :], "d2")
+        group(dad_grouped, 2, d2)
+        a_turned.append(turn_scaled(1))
+        scale_both(3)
+        d3 = turn(dad[:, 3, :], "d3")
+        group(dad_grouped, 3, d3)
         quantise_x(0)
-        scale(2)
-        nc.scalar.copy(out=w_grouped[:], in_=w_rows[:].rearrange("p t o -> p o t"))
-        group(dad_grouped, 0, dad_turned[0])
-        group(dad_grouped, 1, dad_turned[1])
         quantise_x(1)
         quantise(w_codes[:], w_scales[:], w_grouped[:])
-        dad_turned.append(turn(dad[:, 2, :], "d2"))
-        group(dad_grouped, 2, dad_turned[2])
-        scale(3)
+        scale_columns(0, a_turned[0])
+        scale_columns(1, a_turned[1])
 
         support = psum.tile([P, CHUNKS, DOUT], F32, tag="bank")
         for c in range(CHUNKS):
@@ -161,16 +192,14 @@ def tile_crossviewgcn_layer1_s_kernel(tc, inp, weight, out):
                 start=True,
                 stop=True,
             )
-        dad_turned.append(turn(dad[:, 3, :], "d3"))
         nc.scalar.copy(out=s_grouped[:], in_=support[:].rearrange("p t o -> p o t"))
-        group(dad_grouped, 3, dad_turned[3])
+        quantise(s_codes[:], s_scales[:], s_grouped[:])
+        quantise_dad(2)
+        quantise_dad(3)
         quantise_dad(0)
         quantise_dad(1)
-        quantise_dad(2)
-        quantise(s_codes[:], s_scales[:], s_grouped[:])
-        quantise_dad(3)
 
-        for c in range(CHUNKS):
+        for c in (2, 3, 0, 1):
             rows = slice(c * P, (c + 1) * P)
             product = psum.tile([P, DOUT], F32, tag="bank")
             nc.tensor.matmul_mx(
@@ -182,7 +211,7 @@ def tile_crossviewgcn_layer1_s_kernel(tc, inp, weight, out):
                 start=True,
                 stop=True,
             )
-            if c == CHUNKS - 1:
+            if c == 1:
                 nc.vector.tensor_copy(out=result[:, c, :], in_=product[:])
             else:
                 nc.scalar.copy(out=result[:, c, :], in_=product[:])

@@ -20,6 +20,8 @@ CHUNKS = NODES // P
 HALF = NODES // 2
 HALVES = 2
 
+BLOCK = (0, 2, 1, 3)
+
 FLOPS = 2 * NODES * FEATS * DOUT + 2 * NODES * NODES * DOUT
 
 
@@ -61,7 +63,7 @@ def tile_crossviewgcn_layer1_s_kernel(tc, inp, weight, out):
             for t in range(CHUNKS):
                 nc.tensor.matmul(
                     out=colsum[:, t : t + 1],
-                    lhsT=a0[:, c, t * P : (t + 1) * P],
+                    lhsT=a0[:, c, BLOCK[t] * P : (BLOCK[t] + 1) * P],
                     rhs=ones[:],
                     start=(c == 0 and t == 0),
                     stop=(c == CHUNKS - 1 and t == CHUNKS - 1),
@@ -92,6 +94,7 @@ def tile_crossviewgcn_layer1_s_kernel(tc, inp, weight, out):
         dad_codes = keep.tile([P, NODES], U32, align_bytes=64)
         dad_scales = keep.tile([P, NODES], U8, align_bytes=64)
         row_scaled = keep.tile([P, 2, NODES], F32)
+        a_columns = keep.tile([P, P, PACK], F32)
         result = keep.tile([P, CHUNKS, DOUT], F32)
 
         def quantise(codes, scales, grouped):
@@ -113,13 +116,13 @@ def tile_crossviewgcn_layer1_s_kernel(tc, inp, weight, out):
 
         def scale_rows(c):
             nc.vector.tensor_scalar(
-                out=row_scaled[:, c, :], in0=a_f32[:, c, :], scalar1=r[:, c : c + 1], scalar2=None, op0=ALU.mult
+                out=row_scaled[:, c, :], in0=a_f32[:, c, :], scalar1=r[:, BLOCK[c] : BLOCK[c] + 1], scalar2=None, op0=ALU.mult
             )
 
         def turn_scaled(c):
             flipped = psum.tile([P, PACK, P], F32, tag="bank", name="a%d" % c)
             for t in range(PACK):
-                nc.tensor.transpose(flipped[:, t, :], row_scaled[:, c, t * P : (t + 1) * P], ident[:])
+                nc.tensor.transpose(flipped[:, t, :], row_scaled[:, c, BLOCK[t] * P : (BLOCK[t] + 1) * P], ident[:])
             return flipped
 
         def scale_columns(c, flipped):
@@ -131,16 +134,14 @@ def tile_crossviewgcn_layer1_s_kernel(tc, inp, weight, out):
             )
 
         def scale_both(c):
-            for u in range(2):
-                columns = slice(u * HALF, (u + 1) * HALF)
-                nc.vector.scalar_tensor_tensor(
-                    out=dad[:, c, columns].rearrange("p (k e) -> p k e", e=2),
-                    in0=a_f32[:, c, columns].rearrange("p (e k) -> p k e", e=2),
-                    scalar=r[:, c : c + 1],
-                    in1=r_row[:, columns].rearrange("p (e k) -> p k e", e=2),
-                    op0=ALU.mult,
-                    op1=ALU.mult,
-                )
+            nc.vector.scalar_tensor_tensor(
+                out=dad[:, c, :].rearrange("p (m e) -> p m e", e=2),
+                in0=a_f32[:, c, :].rearrange("p (e m) -> p m e", e=2),
+                scalar=r[:, BLOCK[c] : BLOCK[c] + 1],
+                in1=r_row[:].rearrange("p (e m) -> p m e", e=2),
+                op0=ALU.mult,
+                op1=ALU.mult,
+            )
 
         def quantise_x(h):
             nodes = slice(h * HALF, (h + 1) * HALF)
@@ -152,10 +153,14 @@ def tile_crossviewgcn_layer1_s_kernel(tc, inp, weight, out):
 
         scale_rows(0)
         scale_rows(1)
+        x_turned = [turn(x[:, 0, :], "x0")]
         r_row = psum.tile([P, NODES], F32, tag="bank")
         for t in range(CHUNKS):
-            nc.tensor.transpose(r_row[:, t * P : (t + 1) * P], r[:, t : t + 1].to_broadcast([P, P]), ident[:])
-        x_turned = [turn(x[:, c, :], "x%d" % c) for c in range(CHUNKS)]
+            nc.tensor.transpose(
+                r_row[:, BLOCK[t] * P : (BLOCK[t] + 1) * P], r[:, t : t + 1].to_broadcast([P, P]), ident[:]
+            )
+        for c in range(1, CHUNKS):
+            x_turned.append(turn(x[:, c, :], "x%d" % c))
         for c in range(CHUNKS):
             group(x_grouped, c, x_turned[c])
         nc.gpsimd.tensor_scalar(
@@ -167,24 +172,28 @@ def tile_crossviewgcn_layer1_s_kernel(tc, inp, weight, out):
             op1=ALU.add,
         )
         a_turned = [turn_scaled(0)]
+        nc.scalar.copy(out=a_columns[:], in_=a_turned[0][:].rearrange("p t i -> p i t"))
+        for h in range(2):
+            rows = slice(h * P // 2, (h + 1) * P // 2)
+            nc.gpsimd.tensor_tensor(
+                out=dad_grouped[:, rows, :],
+                in0=a_columns[:, rows, :],
+                in1=r[:].unsqueeze(1).to_broadcast([P, P // 2, PACK]),
+                op=ALU.mult,
+            )
         scale_both(2)
         d2 = turn(dad[:, 2, :], "d2")
         group(dad_grouped, 2, d2)
-        a_turned.append(turn_scaled(1))
-        scale_both(3)
-        d3 = turn(dad[:, 3, :], "d3")
-        group(dad_grouped, 3, d3)
         quantise_x(0)
-        quantise_x(1)
         quantise(w_codes[:], w_scales[:], w_grouped[:])
-        scale_columns(0, a_turned[0])
-        scale_columns(1, a_turned[1])
+        quantise_x(1)
+        a_turned.append(turn_scaled(1))
 
         support = psum.tile([P, CHUNKS, DOUT], F32, tag="bank")
         for c in range(CHUNKS):
             nodes = slice(c * P, (c + 1) * P)
             nc.tensor.matmul_mx(
-                out=support[:, c, :],
+                out=support[:, BLOCK[c], :],
                 lhsT=x_codes[:, nodes].bitcast(FP8X4),
                 lhsT_scale=x_scales[:, nodes],
                 rhs=w_codes[:].bitcast(FP8X4),
@@ -193,13 +202,17 @@ def tile_crossviewgcn_layer1_s_kernel(tc, inp, weight, out):
                 stop=True,
             )
         nc.scalar.copy(out=s_grouped[:], in_=support[:].rearrange("p t o -> p o t"))
-        quantise(s_codes[:], s_scales[:], s_grouped[:])
+        scale_both(3)
+        d3 = turn(dad[:, 3, :], "d3")
+        group(dad_grouped, 3, d3)
+        scale_columns(1, a_turned[1])
         quantise_dad(2)
+        quantise(s_codes[:], s_scales[:], s_grouped[:])
+        quantise_dad(1)
         quantise_dad(3)
         quantise_dad(0)
-        quantise_dad(1)
 
-        for c in (2, 3, 0, 1):
+        for c in (2, 1, 3, 0):
             rows = slice(c * P, (c + 1) * P)
             product = psum.tile([P, DOUT], F32, tag="bank")
             nc.tensor.matmul_mx(
@@ -211,7 +224,7 @@ def tile_crossviewgcn_layer1_s_kernel(tc, inp, weight, out):
                 start=True,
                 stop=True,
             )
-            if c == 1:
+            if c == 0:
                 nc.vector.tensor_copy(out=result[:, c, :], in_=product[:])
             else:
                 nc.scalar.copy(out=result[:, c, :], in_=product[:])

@@ -93,7 +93,7 @@ def tile_crossviewgcn_layer1_s_kernel(tc, inp, weight, out):
         dad_grouped = keep.tile([P, NODES, PACK], BF16, align_bytes=64)
         dad_codes = keep.tile([P, NODES], U32, align_bytes=64)
         dad_scales = keep.tile([P, NODES], U8, align_bytes=64)
-        row_scaled = keep.tile([P, 2, NODES], F32)
+        row_scaled = keep.tile([P, CHUNKS, NODES], F32)
         a_columns = keep.tile([P, P, PACK], F32)
         result = keep.tile([P, CHUNKS, DOUT], F32)
 
@@ -153,6 +153,9 @@ def tile_crossviewgcn_layer1_s_kernel(tc, inp, weight, out):
 
         scale_rows(0)
         scale_rows(1)
+        nc.scalar.activation(
+            out=row_scaled[:, 3, :], in_=a_f32[:, 3, :], func=ACT.Copy, scale=r[:, BLOCK[3] : BLOCK[3] + 1]
+        )
         x_turned = [turn(x[:, 0, :], "x0")]
         r_row = psum.tile([P, NODES], F32, tag="bank")
         for t in range(CHUNKS):
@@ -171,7 +174,7 @@ def tile_crossviewgcn_layer1_s_kernel(tc, inp, weight, out):
             op0=ALU.mult,
             op1=ALU.add,
         )
-        a_turned = [turn_scaled(0)]
+        a_turned = {0: turn_scaled(0), 3: turn_scaled(3)}
         nc.scalar.copy(out=a_columns[:], in_=a_turned[0][:].rearrange("p t i -> p i t"))
         for h in range(2):
             rows = slice(h * P // 2, (h + 1) * P // 2)
@@ -187,7 +190,7 @@ def tile_crossviewgcn_layer1_s_kernel(tc, inp, weight, out):
         quantise_x(0)
         quantise(w_codes[:], w_scales[:], w_grouped[:])
         quantise_x(1)
-        a_turned.append(turn_scaled(1))
+        a_turned[1] = turn_scaled(1)
 
         support = psum.tile([P, CHUNKS, DOUT], F32, tag="bank")
         for c in range(CHUNKS):
@@ -202,9 +205,7 @@ def tile_crossviewgcn_layer1_s_kernel(tc, inp, weight, out):
                 stop=True,
             )
         nc.scalar.copy(out=s_grouped[:], in_=support[:].rearrange("p t o -> p o t"))
-        scale_both(3)
-        d3 = turn(dad[:, 3, :], "d3")
-        group(dad_grouped, 3, d3)
+        scale_columns(3, a_turned[3])
         scale_columns(1, a_turned[1])
         quantise_dad(2)
         quantise(s_codes[:], s_scales[:], s_grouped[:])

@@ -47,8 +47,15 @@ def tile_crossviewgcn_layer1_s_kernel(tc, inp, weight, out):
         ident = keep.tile([P, P], F32)
         make_identity(nc, ident[:])
         warm_bank = psum.tile([P, P], F32, tag="bank")
-        for i in range(3):
-            nc.tensor.matmul(out=warm_bank[:], lhsT=ident[:], rhs=ident[:], start=True, stop=True)
+
+        def dummy_product(width):
+            nc.tensor.matmul(
+                out=warm_bank[:, 0:width], lhsT=ident[:], rhs=ident[:, 0:width], start=True, stop=True
+            )
+
+        dummy_product(P)
+        dummy_product(P)
+        dummy_product(P // 2)
         eye_wide = keep.tile([P, 3 * P], BF16)
         nc.vector.memset(eye_wide[:], 0.0)
         nc.vector.tensor_copy(out=eye_wide[:, P : 2 * P], in_=ident[:])
@@ -76,6 +83,8 @@ def tile_crossviewgcn_layer1_s_kernel(tc, inp, weight, out):
             )
             nc.scalar.copy(out=a_f32[:, c, without], in_=a0[:, c, without])
             nc.sync.dma_start(out=out[c * P : (c + 1) * P, DOUT : DOUT + NODES], in_=a_f32[:, c, :])
+
+        dummy_product(P // 2)
 
         r = keep.tile([P, CHUNKS], F32)
         nc.scalar.activation(out=r[:], in_=colsum[:], func=ACT.Abs_reciprocal_sqrt, bias=1.0)

@@ -184,9 +184,9 @@ def tile_crossviewgcn_layer1_s_kernel(tc, inp, weight, out):
             op1=ALU.add,
         )
         a_turned = {0: turn_scaled(0), 3: turn_scaled(3)}
-        nc.scalar.copy(out=a_columns[:], in_=a_turned[0][:].rearrange("p t i -> p i t"))
         for h in range(2):
             rows = slice(h * P // 2, (h + 1) * P // 2)
+            nc.scalar.copy(out=a_columns[:, rows, :], in_=a_turned[0][:, :, rows].rearrange("p t i -> p i t"))
             nc.gpsimd.tensor_tensor(
                 out=dad_grouped[:, rows, :],
                 in0=a_columns[:, rows, :],
@@ -234,8 +234,9 @@ def tile_crossviewgcn_layer1_s_kernel(tc, inp, weight, out):
                 start=True,
                 stop=True,
             )
-            if c == 0:
+            if c == 1:
                 nc.vector.tensor_copy(out=result[:, c, :], in_=product[:])
             else:
                 nc.scalar.copy(out=result[:, c, :], in_=product[:])
-            nc.sync.dma_start(out=out[rows, 0:DOUT], in_=result[:, c, :])
+            queue = nc.scalar if c == 0 else nc.sync
+            queue.dma_start(out=out[rows, 0:DOUT], in_=result[:, c, :])

from contextlib import ExitStack

import concourse.mybir as mybir
from concourse.masks import make_identity

F32 = mybir.dt.float32
BF16 = mybir.dt.bfloat16
U32 = mybir.dt.uint32
U8 = mybir.dt.uint8
FP8X4 = mybir.dt.float8_e4m3fn_x4
ALU = mybir.AluOpType
ACT = mybir.ActivationFunctionType

P = 128
PACK = 4
NODES = 512
FEATS = 512
DOUT = 128
CHUNKS = NODES // P
HALF = NODES // 2
HALVES = 2

BLOCK = (0, 2, 1, 3)

FLOPS = 2 * NODES * FEATS * DOUT + 2 * NODES * NODES * DOUT


def tile_crossviewgcn_layer1_s_kernel(tc, inp, weight, out):
    nc = tc.nc
    with ExitStack() as ctx:
        keep = ctx.enter_context(tc.tile_pool(name="keep", bufs=1))
        psum = ctx.enter_context(tc.psum_pool(name="psum", bufs=8))
        ctx.enter_context(tc.manual_schedule())

        a0 = keep.tile([P, CHUNKS, NODES], BF16)
        for c in range(CHUNKS):
            nc.sync.dma_start(out=a0[:, c, :], in_=inp[c * P : (c + 1) * P, FEATS : FEATS + NODES])
        x = keep.tile([P, CHUNKS, FEATS], BF16)
        for c in range(CHUNKS):
            nc.sync.dma_start(out=x[:, c, :], in_=inp[c * P : (c + 1) * P, 0:FEATS])
        w_rows = keep.tile([P, PACK, DOUT], BF16)
        nc.sync.dma_start(
            out=w_rows[:].rearrange("p (u e) o -> p u (e o)", u=2),
            in_=weight.rearrange("(u p e) o -> p u (e o)", u=2, e=2),
        )

        ident = keep.tile([P, P], F32)
        make_identity(nc, ident[:])
        warm_bank = psum.tile([P, P], F32, tag="bank")

        def dummy_product(width):
            nc.tensor.matmul(
                out=warm_bank[:, 0:width], lhsT=ident[:], rhs=ident[:, 0:width], start=True, stop=True
            )

        dummy_product(P)
        dummy_product(P)
        dummy_product(P // 2)
        eye_wide = keep.tile([P, 3 * P], BF16)
        nc.vector.memset(eye_wide[:], 0.0)
        nc.vector.tensor_copy(out=eye_wide[:, P : 2 * P], in_=ident[:])
        ones = keep.tile([P, 1], BF16)
        nc.vector.memset(ones[:], 1.0)
        warm = keep.tile([P, 1], F32)
        nc.scalar.activation(out=warm[:], in_=ones[:], func=ACT.Abs_reciprocal_sqrt)

        colsum = psum.tile([P, CHUNKS], F32, tag="bank")
        a_f32 = keep.tile([P, CHUNKS, NODES], F32)
        for c in range(CHUNKS):
            for t in range(CHUNKS):
                nc.tensor.matmul(
                    out=colsum[:, t : t + 1],
                    lhsT=a0[:, c, BLOCK[t] * P : (BLOCK[t] + 1) * P],
                    rhs=ones[:],
                    start=(c == 0 and t == 0),
                    stop=(c == CHUNKS - 1 and t == CHUNKS - 1),
                )
            with_diag = slice((c // 2) * HALF, (c // 2 + 1) * HALF)
            without = slice((1 - c // 2) * HALF, (2 - c // 2) * HALF)
            first = (1 - c % 2) * P
            nc.vector.tensor_tensor(
                out=a_f32[:, c, with_diag], in0=a0[:, c, with_diag], in1=eye_wide[:, first : first + HALF], op=ALU.add
            )
            nc.scalar.copy(out=a_f32[:, c, without], in_=a0[:, c, without])
            nc.sync.dma_start(out=out[c * P : (c + 1) * P, DOUT : DOUT + NODES], in_=a_f32[:, c, :])

        dummy_product(P // 2)

        r = keep.tile([P, CHUNKS], F32)
        nc.scalar.activation(out=r[:], in_=colsum[:], func=ACT.Abs_reciprocal_sqrt, bias=1.0)

        w_grouped = keep.tile([P, DOUT, PACK], BF16, align_bytes=64)
        w_codes = keep.tile([P, DOUT], U32, align_bytes=64)
        w_scales = keep.tile([P, DOUT], U8, align_bytes=64)
        x_grouped = keep.tile([P, NODES, PACK], BF16, align_bytes=64)
        x_codes = keep.tile([P, NODES], U32, align_bytes=64)
        x_scales = keep.tile([P, NODES], U8, align_bytes=64)
        s_grouped = keep.tile([P, DOUT, PACK], BF16, align_bytes=64)
        s_codes = keep.tile([P, DOUT], U32, align_bytes=64)
        s_scales = keep.tile([P, DOUT], U8, align_bytes=64)
        dad = keep.tile([P, CHUNKS, NODES], BF16, align_bytes=64)
        dad_grouped = keep.tile([P, NODES, PACK], BF16, align_bytes=64)
        dad_codes = keep.tile([P, NODES], U32, align_bytes=64)
        dad_scales = keep.tile([P, NODES], U8, align_bytes=64)
        row_scaled = keep.tile([P, CHUNKS, NODES], F32)
        a_columns = keep.tile([P, P, PACK], F32)
        result = keep.tile([P, CHUNKS, DOUT], F32)

        def quantise(codes, scales, grouped):
            nc.vector.quantize_mx(
                out=codes.bitcast(FP8X4), scales=scales, in_=grouped.rearrange("p w t -> p (w t)")
            )

        def turn(rows, name):
            flipped = psum.tile([P, 2, P], F32, tag="bank", name=name)
            words = rows.bitcast(F32)
            for u in range(2):
                nc.tensor.transpose(flipped[:, u, :], words[:, u * P : (u + 1) * P], ident[:])
            return flipped

        def group(grouped, c, flipped):
            nc.scalar.copy(
                out=grouped[:, c * P : (c + 1) * P, :].bitcast(F32), in_=flipped[:].rearrange("p u n -> p n u")
            )

        def scale_rows(c):
            nc.vector.tensor_scalar(
                out=row_scaled[:, c, :], in0=a_f32[:, c, :], scalar1=r[:, BLOCK[c] : BLOCK[c] + 1], scalar2=None, op0=ALU.mult
            )

        def turn_scaled(c):
            flipped = psum.tile([P, PACK, P], F32, tag="bank", name="a%d" % c)
            for t in range(PACK):
                nc.tensor.transpose(flipped[:, t, :], row_scaled[:, c, BLOCK[t] * P : (BLOCK[t] + 1) * P], ident[:])
            return flipped

        def scale_columns(c, flipped):
            nc.vector.tensor_tensor(
                out=dad_grouped[:, c * P : (c + 1) * P, :],
                in0=flipped[:].rearrange("p t i -> p i t"),
                in1=r[:].unsqueeze(1).to_broadcast([P, P, PACK]),
                op=ALU.mult,
            )

        def scale_both(c):
            nc.vector.scalar_tensor_tensor(
                out=dad[:, c, :].rearrange("p (m e) -> p m e", e=2),
                in0=a_f32[:, c, :].rearrange("p (e m) -> p m e", e=2),
                scalar=r[:, BLOCK[c] : BLOCK[c] + 1],
                in1=r_row[:].rearrange("p (e m) -> p m e", e=2),
                op0=ALU.mult,
                op1=ALU.mult,
            )

        def quantise_x(h):
            nodes = slice(h * HALF, (h + 1) * HALF)
            quantise(x_codes[:, nodes], x_scales[:, nodes], x_grouped[:, nodes, :])

        def quantise_dad(c):
            rows = slice(c * P, (c + 1) * P)
            quantise(dad_codes[:, rows], dad_scales[:, rows], dad_grouped[:, rows, :])

        scale_rows(0)
        scale_rows(1)
        nc.scalar.activation(
            out=row_scaled[:, 3, :], in_=a_f32[:, 3, :], func=ACT.Copy, scale=r[:, BLOCK[3] : BLOCK[3] + 1]
        )
        x_turned = [turn(x[:, 0, :], "x0")]
        r_row = psum.tile([P, NODES], F32, tag="bank")
        for t in range(CHUNKS):
            nc.tensor.transpose(
                r_row[:, BLOCK[t] * P : (BLOCK[t] + 1) * P], r[:, t : t + 1].to_broadcast([P, P]), ident[:]
            )
        for c in range(1, CHUNKS):
            x_turned.append(turn(x[:, c, :], "x%d" % c))
        for c in range(CHUNKS):
            group(x_grouped, c, x_turned[c])
        nc.gpsimd.tensor_scalar(
            out=w_grouped[:],
            in0=w_rows[:].rearrange("p t o -> p o t"),
            scalar1=1.0,
            scalar2=0.0,
            op0=ALU.mult,
            op1=ALU.add,
        )
        a_turned = {0: turn_scaled(0), 3: turn_scaled(3)}
        for h in range(2):
            rows = slice(h * P // 2, (h + 1) * P // 2)
            nc.scalar.copy(out=a_columns[:, rows, :], in_=a_turned[0][:, :, rows].rearrange("p t i -> p i t"))
            nc.gpsimd.tensor_tensor(
                out=dad_grouped[:, rows, :],
                in0=a_columns[:, rows, :],
                in1=r[:].unsqueeze(1).to_broadcast([P, P // 2, PACK]),
                op=ALU.mult,
            )
        scale_both(2)
        d2 = turn(dad[:, 2, :], "d2")
        group(dad_grouped, 2, d2)
        quantise_x(0)
        quantise(w_codes[:], w_scales[:], w_grouped[:])
        quantise_x(1)
        a_turned[1] = turn_scaled(1)

        support = psum.tile([P, CHUNKS, DOUT], F32, tag="bank")
        for c in range(CHUNKS):
            nodes = slice(c * P, (c + 1) * P)
            nc.tensor.matmul_mx(
                out=support[:, BLOCK[c], :],
                lhsT=x_codes[:, nodes].bitcast(FP8X4),
                lhsT_scale=x_scales[:, nodes],
                rhs=w_codes[:].bitcast(FP8X4),
                rhs_scale=w_scales[:],
                start=True,
                stop=True,
            )
        nc.scalar.copy(out=s_grouped[:], in_=support[:].rearrange("p t o -> p o t"))
        scale_columns(3, a_turned[3])
        scale_columns(1, a_turned[1])
        quantise_dad(2)
        quantise(s_codes[:], s_scales[:], s_grouped[:])
        quantise_dad(1)
        quantise_dad(3)
        quantise_dad(0)

        for c in (2, 1, 3, 0):
            rows = slice(c * P, (c + 1) * P)
            product = psum.tile([P, DOUT], F32, tag="bank")
            nc.tensor.matmul_mx(
                out=product[:],
                lhsT=dad_codes[:, rows].bitcast(FP8X4),
                lhsT_scale=dad_scales[:, rows],
                rhs=s_codes[:].bitcast(FP8X4),
                rhs_scale=s_scales[:],
                start=True,
                stop=True,
            )
            if c == 1:
                nc.vector.tensor_copy(out=result[:, c, :], in_=product[:])
            else:
                nc.scalar.copy(out=result[:, c, :], in_=product[:])
            queue = nc.scalar if c == 0 else nc.sync
            queue.dma_start(out=out[rows, 0:DOUT], in_=result[:, c, :])
